import numpy as np
import ml_dtypes


def mxq(x, axis, fmt="e4m3"):
    dtype, down = {"e4m3": (ml_dtypes.float8_e4m3fn, 7), "e5m2": (ml_dtypes.float8_e5m2, 14)}[fmt]
    v = np.moveaxis(np.asarray(x, np.float32).astype(ml_dtypes.bfloat16).astype(np.float64), axis, -1)
    blocks = v.reshape(v.shape[:-1] + (-1, 32))
    amax = np.abs(blocks).max(-1, keepdims=True)
    byte = np.maximum(np.where(amax > 0, np.frexp(amax)[1] - 1 + 127, 0) - down, 1)
    scale = np.exp2(byte - 127.0)
    codes = (blocks / scale).astype(np.float32).astype(dtype).astype(np.float64)
    return np.moveaxis((codes * scale).reshape(v.shape), -1, axis)


WIDE = False


def mx_kscale(k):
    if not WIDE:
        return np.ones(k)
    levels = np.array([10, -10, 5, -5, 0])
    if k % 512:
        return np.exp2(np.random.permutation(np.resize(levels, k // 32))).repeat(32)
    a = np.empty((k // 512, 16))
    for p in range(k // 512):
        a[p, :8] = np.random.permutation(np.resize(levels, 8))
        for g in range(8):
            far = levels[np.abs(levels - a[p, g]) >= 10]
            a[p, g + 8] = far[np.random.randint(len(far))]
    return np.exp2(a.ravel()).repeat(32)


BF16 = ml_dtypes.bfloat16


def bf(x):
    return np.asarray(x, np.float32).astype(BF16)


def f64(x):
    return np.asarray(x).astype(np.float64)


B, T, S, H, C, CO, W = 2, 128, 16, 8, 1024, 1024, 5
HD = C // H


def setup_inputs():
    t = mx_kscale(C)
    i = np.arange(T)
    band = np.abs(i[:, None] - i[None, :]) <= W
    e = np.exp(np.random.standard_normal((B, H, S, T, T))) * band
    return {"attn": bf(e / e.sum(-1, keepdims=True)),
            "v": bf(np.random.standard_normal((B, T, S, H, HD)) * t.reshape(H, HD)),
            "W_out": bf(np.random.standard_normal((C, CO)) / np.sqrt(C) / t[:, None])}


def reference(attn, v, W_out):
    ctx = f64(attn) @ f64(v).transpose(0, 3, 2, 1, 4)
    ctx = ctx.transpose(0, 3, 2, 1, 4).reshape(B * T * S, C)
    return (mxq(ctx, 1, "e4m3") @ mxq(f64(W_out), 0, "e4m3")).reshape(B, T * S, CO)

@@ -1,0 +1,209 @@
+from contextlib import ExitStack
+
+import concourse.masks as masks
+import concourse.mybir as mybir
+
+BF16 = mybir.dt.bfloat16
+F32 = mybir.dt.float32
+U32 = mybir.dt.uint32
+U8 = mybir.dt.uint8
+FP8X4 = mybir.dt.float8_e4m3fn_x4
+
+P = 128
+B, S, H, CO = 2, 16, 8, 1024
+PACK = 4
+PASSES = 2
+HEADS = H // PASSES
+BANK_COLS = 512
+COL_HALVES = CO // BANK_COLS
+J = 8
+TH = P // J
+S_GROUP = P // TH
+GROUPS = B * S // S_GROUP
+S_PAIR = 2
+STEPS = B * S
+LAG = 2
+AHEAD = 8
+
+FLOPS = 2 * B * H * S * P * P * P + 2 * B * S * P * H * P * CO
+
+
+def tile_localtemporalattention_pa_kernel(tc, attn, v, W_out, out):
+    nc = tc.nc
+    with ExitStack() as stack:
+        stack.enter_context(tc.manual_schedule())
+        const = stack.enter_context(tc.tile_pool(name="const", bufs=1))
+        attn_pool = stack.enter_context(tc.tile_pool(name="attn", bufs=AHEAD + 4))
+        v_pool = stack.enter_context(tc.tile_pool(name="v", bufs=AHEAD // S_PAIR + 2))
+        flipped_pool = stack.enter_context(tc.tile_pool(name="flipped", bufs=2 * H))
+        ctx_pool = stack.enter_context(tc.tile_pool(name="ctx", bufs=3))
+        grouped_pool = stack.enter_context(tc.tile_pool(name="grouped", bufs=3))
+        code_pool = stack.enter_context(tc.tile_pool(name="codes", bufs=LAG + 2))
+        out_pool = stack.enter_context(tc.tile_pool(name="out", bufs=6))
+        psum = stack.enter_context(tc.psum_pool(name="psum", bufs=8))
+
+        attn_rows = {}
+        v_rows = {}
+        attn_t = {}
+        ctx_rows = {}
+        ctx_grouped = {}
+        ctx_codes = {}
+        ctx_scales = {}
+
+        def load_attn(group, h):
+            b, s_half = divmod(group, S // S_GROUP)
+            rows = attn_pool.tile([P, J * P], BF16, name="attn_rows")
+            nc.sync.dma_start(
+                out=rows[:],
+                in_=attn[b, h, S_GROUP * s_half : S_GROUP * (s_half + 1)].rearrange(
+                    "s (th j) u -> (s th) (j u)", j=J
+                ),
+            )
+            attn_rows[(group, h)] = rows
+
+        def load_for(step):
+            if step >= STEPS:
+                return
+            if step % S_PAIR == 0:
+                b, s = divmod(step, S)
+                rows = v_pool.tile([P, S_PAIR, H, P], BF16, name="v_rows")
+                nc.sync.dma_start(out=rows[:], in_=v[b, :, s : s + S_PAIR])
+                v_rows[step // S_PAIR] = rows
+            group, h = divmod(step, S_GROUP)
+            if group + 1 < GROUPS:
+                load_attn(group + 1, h)
+
+        def flip(group, h, copy):
+            bank = psum.tile([P, J, P], BF16, name="flip_bank", tag="bank")
+            rows = attn_rows[(group, h)]
+            for j in range(J):
+                nc.tensor.transpose(bank[:, j, :], rows[:, P * j : P * (j + 1)], ident[:])
+            flipped = flipped_pool.tile([P, S_GROUP, P], BF16, name="flipped")
+            copy(
+                out=flipped[:].rearrange("u s (j th) -> u s j th", j=J),
+                in_=bank[:].rearrange("u j (s th) -> u s j th", s=S_GROUP),
+            )
+            attn_t[(group, h)] = flipped
+
+        def mix(step):
+            group, s_local = divmod(step, S_GROUP)
+            values = v_rows[step // S_PAIR]
+            rows = ctx_pool.tile([P, PASSES, PACK // 2, P, 2], BF16, name="ctx_rows", align_bytes=64)
+            for g in range(PASSES):
+                bank = psum.tile([P, HEADS, P], F32, name="ctx_bank", tag="bank")
+                for hh in range(HEADS):
+                    h = HEADS * g + hh
+                    nc.tensor.matmul(
+                        out=bank[:, hh, :],
+                        lhsT=attn_t[(group, h)][:, s_local, :],
+                        rhs=values[:, step % S_PAIR, h, :],
+                        start=True,
+                        stop=True,
+                    )
+                nc.scalar.copy(
+                    out=rows[:, g],
+                    in_=bank[:].rearrange("x hh (q i e) -> x i (hh q) e", i=PACK // 2, e=2),
+                )
+            ctx_rows[step] = rows
+
+        def group_channels(step):
+            words = ctx_rows[step][:].rearrange("x g i p e -> x (g i p e)").bitcast(F32)
+            bank = psum.tile([P, PASSES, PACK // 2, P], F32, name="group_bank", tag="bank")
+            for g in range(PASSES):
+                for i in range(PACK // 2):
+                    k = (PACK // 2) * g + i
+                    nc.tensor.transpose(bank[:, g, i, :], words[:, P * k : P * (k + 1)], in_order[:])
+            grouped = grouped_pool.tile([P, PASSES * P * PACK], BF16, name="ctx_grouped", align_bytes=64)
+            nc.vector.tensor_copy(
+                out=grouped[:].bitcast(F32).rearrange("p (g t i) -> p g t i", g=PASSES, i=PACK // 2),
+                in_=bank[:].rearrange("p g i t -> p g t i"),
+            )
+            ctx_grouped[step] = grouped
+
+        def quantise_ctx(step):
+            codes = code_pool.tile([P, PASSES * P], U32, name="ctx_codes", align_bytes=64)
+            scales = code_pool.tile([P, PASSES * P], U8, name="ctx_scales", align_bytes=64)
+            nc.vector.quantize_mx(
+                out=codes[:].bitcast(FP8X4), scales=scales[:], in_=ctx_grouped[step][:]
+            )
+            ctx_codes[step] = codes
+            ctx_scales[step] = scales
+
+        def project(step):
+            b, s = divmod(step, S)
+            result = out_pool.tile([P, CO], F32, name="result")
+            for half, copy in enumerate((nc.scalar.copy, nc.vector.tensor_copy)):
+                cols = slice(BANK_COLS * half, BANK_COLS * (half + 1))
+                bank = psum.tile([P, BANK_COLS], F32, name="out_bank", tag="bank")
+                for g in range(PASSES):
+                    rows = slice(P * g, P * (g + 1))
+                    nc.tensor.matmul_mx(
+                        out=bank[:],
+                        lhsT=ctx_codes[step][:, rows].bitcast(FP8X4),
+                        lhsT_scale=ctx_scales[step][:, rows],
+                        rhs=w_codes[:, g, cols].bitcast(FP8X4),
+                        rhs_scale=w_scales[:, g, cols],
+                        start=(g == 0),
+                        stop=(g == PASSES - 1),
+                    )
+                copy(out=result[:, cols], in_=bank[:])
+            nc.sync.dma_start(out=out[b].rearrange("(t s) c -> s t c", s=S)[s], in_=result[:])
+
+        w_raw = []
+        for g in range(PASSES):
+            for hh in range(HEADS):
+                load_attn(0, HEADS * g + hh)
+            raw = const.tile([P, PACK, CO], BF16, name="w_raw%d" % g)
+            nc.sync.dma_start(
+                out=raw[:],
+                in_=W_out[PACK * P * g : PACK * P * (g + 1), :].rearrange("(p i) n -> p i n", i=PACK),
+            )
+            w_raw.append(raw)
+
+        ident = const.tile([P, P], BF16, name="ident")
+        masks.make_identity(nc, ident[:])
+        ident_f32 = const.tile([P, P], F32, name="ident_f32")
+        masks.make_identity(nc, ident_f32[:])
+        in_order = const.tile([P, P], F32, name="in_order")
+        nc.gpsimd.tensor_copy(
+            out=in_order[:].rearrange("x (th j) -> x th j", j=J),
+            in_=ident_f32[:].rearrange("x (j th) -> x th j", j=J),
+        )
+
+        w_codes = const.tile([P, PASSES, CO], U32, name="w_codes", align_bytes=64)
+        w_scales = const.tile([P, PASSES, CO], U8, name="w_scales", align_bytes=64)
+        for g in range(PASSES):
+            grouped = const.tile([P, CO, PACK], BF16, name="w_grouped%d" % g, align_bytes=64)
+            for half in range(COL_HALVES):
+                cols = slice(BANK_COLS * half, BANK_COLS * (half + 1))
+                nc.vector.tensor_copy(
+                    out=grouped[:, cols, :].rearrange("p (c n) i -> p c i n", n=4),
+                    in_=w_raw[g][:, :, cols].rearrange("p i (c n) -> p c i n", n=4),
+                )
+            for half in range(COL_HALVES):
+                cols = slice(BANK_COLS * half, BANK_COLS * (half + 1))
+                nc.vector.quantize_mx(
+                    out=w_codes[:, g, cols].bitcast(FP8X4),
+                    scales=w_scales[:, g, cols],
+                    in_=grouped[:, cols, :].rearrange("p n i -> p (n i)"),
+                )
+
+        for h in range(H):
+            flip(0, h, nc.scalar.copy)
+
+        for step in range(AHEAD):
+            load_for(step)
+
+        for step in range(STEPS + LAG):
+            if step >= LAG:
+                quantise_ctx(step - LAG)
+            if step < STEPS:
+                load_for(step + AHEAD)
+                mix(step)
+                group, h = divmod(step, S_GROUP)
+                if group + 1 < GROUPS:
+                    flip(group + 1, h, nc.vector.tensor_copy)
+            if 1 <= step <= STEPS:
+                group_channels(step - 1)
+            if step >= LAG:
+                project(step - LAG)

@@ -17,6 +17,7 @@ HEADS = H // PASSES
 BANK_COLS = 512
 COL_HALVES = CO // BANK_COLS
 J = 8
+K = J // 2
 TH = P // J
 S_GROUP = P // TH
 GROUPS = B * S // S_GROUP
@@ -34,6 +35,7 @@ def tile_localtemporalattention_pa_kernel(tc, attn, v, W_out, out):
         stack.enter_context(tc.manual_schedule())
         const = stack.enter_context(tc.tile_pool(name="const", bufs=1))
         attn_pool = stack.enter_context(tc.tile_pool(name="attn", bufs=AHEAD + 4))
+        pair_pool = stack.enter_context(tc.tile_pool(name="pairs", bufs=8))
         v_pool = stack.enter_context(tc.tile_pool(name="v", bufs=AHEAD // S_PAIR + 2))
         flipped_pool = stack.enter_context(tc.tile_pool(name="flipped", bufs=2 * H))
         ctx_pool = stack.enter_context(tc.tile_pool(name="ctx", bufs=3))
@@ -44,6 +46,7 @@ def tile_localtemporalattention_pa_kernel(tc, attn, v, W_out, out):
 
         attn_rows = {}
         v_rows = {}
+        attn_pairs = {}
         attn_t = {}
         ctx_rows = {}
         ctx_grouped = {}
@@ -73,15 +76,25 @@ def tile_localtemporalattention_pa_kernel(tc, attn, v, W_out, out):
             if group + 1 < GROUPS:
                 load_attn(group + 1, h)
 
+        def pair_frames(group, h):
+            pairs = pair_pool.tile([P, K, P, 2], BF16, name="pairs")
+            nc.vector.tensor_copy(
+                out=pairs[:],
+                in_=attn_rows[(group, h)][:].rearrange("p (k e u) -> p k u e", k=K, e=2),
+            )
+            attn_pairs[(group, h)] = pairs
+
         def flip(group, h, copy):
-            bank = psum.tile([P, J, P], BF16, name="flip_bank", tag="bank")
-            rows = attn_rows[(group, h)]
-            for j in range(J):
-                nc.tensor.transpose(bank[:, j, :], rows[:, P * j : P * (j + 1)], ident[:])
+            bank = psum.tile([P, K, P], F32, name="flip_bank", tag="bank")
+            words = attn_pairs[(group, h)][:].rearrange("p k u e -> p (k u e)").bitcast(F32)
+            for k in range(K):
+                nc.tensor.transpose(bank[:, k, :], words[:, P * k : P * (k + 1)], ident[:])
             flipped = flipped_pool.tile([P, S_GROUP, P], BF16, name="flipped")
             copy(
-                out=flipped[:].rearrange("u s (j th) -> u s j th", j=J),
-                in_=bank[:].rearrange("u j (s th) -> u s j th", s=S_GROUP),
+                out=flipped[:].rearrange("u s t -> u (s t)").bitcast(F32).rearrange(
+                    "u (s th k) -> u s th k", s=S_GROUP, k=K
+                ),
+                in_=bank[:].rearrange("u k (s th) -> u s th k", s=S_GROUP),
             )
             attn_t[(group, h)] = flipped
 
@@ -102,17 +115,17 @@ def tile_localtemporalattention_pa_kernel(tc, attn, v, W_out, out):
                     )
                 nc.scalar.copy(
                     out=rows[:, g],
-                    in_=bank[:].rearrange("x hh (q i e) -> x i (hh q) e", i=PACK // 2, e=2),
+                    in_=bank[:].rearrange("t hh (q i e) -> t i (hh q) e", i=PACK // 2, e=2),
                 )
             ctx_rows[step] = rows
 
         def group_channels(step):
-            words = ctx_rows[step][:].rearrange("x g i p e -> x (g i p e)").bitcast(F32)
+            words = ctx_rows[step][:].rearrange("t g i p e -> t (g i p e)").bitcast(F32)
             bank = psum.tile([P, PASSES, PACK // 2, P], F32, name="group_bank", tag="bank")
             for g in range(PASSES):
                 for i in range(PACK // 2):
                     k = (PACK // 2) * g + i
-                    nc.tensor.transpose(bank[:, g, i, :], words[:, P * k : P * (k + 1)], in_order[:])
+                    nc.tensor.transpose(bank[:, g, i, :], words[:, P * k : P * (k + 1)], ident[:])
             grouped = grouped_pool.tile([P, PASSES * P * PACK], BF16, name="ctx_grouped", align_bytes=64)
             nc.vector.tensor_copy(
                 out=grouped[:].bitcast(F32).rearrange("p (g t i) -> p g t i", g=PASSES, i=PACK // 2),
@@ -132,7 +145,7 @@ def tile_localtemporalattention_pa_kernel(tc, attn, v, W_out, out):
         def project(step):
             b, s = divmod(step, S)
             result = out_pool.tile([P, CO], F32, name="result")
-            for half, copy in enumerate((nc.scalar.copy, nc.vector.tensor_copy)):
+            for half in range(COL_HALVES):
                 cols = slice(BANK_COLS * half, BANK_COLS * (half + 1))
                 bank = psum.tile([P, BANK_COLS], F32, name="out_bank", tag="bank")
                 for g in range(PASSES):
@@ -146,7 +159,7 @@ def tile_localtemporalattention_pa_kernel(tc, attn, v, W_out, out):
                         start=(g == 0),
                         stop=(g == PASSES - 1),
                     )
-                copy(out=result[:, cols], in_=bank[:])
+                nc.scalar.copy(out=result[:, cols], in_=bank[:])
             nc.sync.dma_start(out=out[b].rearrange("(t s) c -> s t c", s=S)[s], in_=result[:])
 
         w_raw = []
@@ -160,19 +173,14 @@ def tile_localtemporalattention_pa_kernel(tc, attn, v, W_out, out):
             )
             w_raw.append(raw)
 
-        ident = const.tile([P, P], BF16, name="ident")
+        ident = const.tile([P, P], F32, name="ident")
         masks.make_identity(nc, ident[:])
-        ident_f32 = const.tile([P, P], F32, name="ident_f32")
-        masks.make_identity(nc, ident_f32[:])
-        in_order = const.tile([P, P], F32, name="in_order")
-        nc.gpsimd.tensor_copy(
-            out=in_order[:].rearrange("x (th j) -> x th j", j=J),
-            in_=ident_f32[:].rearrange("x (j th) -> x th j", j=J),
-        )
 
         w_codes = const.tile([P, PASSES, CO], U32, name="w_codes", align_bytes=64)
         w_scales = const.tile([P, PASSES, CO], U8, name="w_scales", align_bytes=64)
         for g in range(PASSES):
+            for hh in range(HEADS):
+                pair_frames(0, HEADS * g + hh)
             grouped = const.tile([P, CO, PACK], BF16, name="w_grouped%d" % g, align_bytes=64)
             for half in range(COL_HALVES):
                 cols = slice(BANK_COLS * half, BANK_COLS * (half + 1))
@@ -193,6 +201,7 @@ def tile_localtemporalattention_pa_kernel(tc, attn, v, W_out, out):
 
         for step in range(AHEAD):
             load_for(step)
+        pair_frames(1, 0)
 
         for step in range(STEPS + LAG):
             if step >= LAG:
@@ -200,9 +209,10 @@ def tile_localtemporalattention_pa_kernel(tc, attn, v, W_out, out):
             if step < STEPS:
                 load_for(step + AHEAD)
                 mix(step)
-                group, h = divmod(step, S_GROUP)
-                if group + 1 < GROUPS:
-                    flip(group + 1, h, nc.vector.tensor_copy)
+                if step + S_GROUP < STEPS:
+                    flip(*divmod(step + S_GROUP, S_GROUP), nc.vector.tensor_copy)
+                if step + 1 + S_GROUP < STEPS:
+                    pair_frames(*divmod(step + 1 + S_GROUP, S_GROUP))
             if 1 <= step <= STEPS:
                 group_channels(step - 1)
             if step >= LAG:

@@ -16,15 +16,17 @@ PASSES = 2
 HEADS = H // PASSES
 BANK_COLS = 512
 COL_HALVES = CO // BANK_COLS
-J = 8
+GROUP = 4
+TH = P // GROUP
+J = P // TH
 K = J // 2
-TH = P // J
-S_GROUP = P // TH
-GROUPS = B * S // S_GROUP
-S_PAIR = 2
+UNIT = 2
+UNITS = H // UNIT
 STEPS = B * S
+GROUPS = STEPS // GROUP
 LAG = 2
-AHEAD = 8
+PLAIN_GROUPS = 2
+AHEAD = 3
 
 FLOPS = 2 * B * H * S * P * P * P + 2 * B * S * P * H * P * CO
 
@@ -34,10 +36,10 @@ def tile_localtemporalattention_pa_kernel(tc, attn, v, W_out, out):
     with ExitStack() as stack:
         stack.enter_context(tc.manual_schedule())
         const = stack.enter_context(tc.tile_pool(name="const", bufs=1))
-        attn_pool = stack.enter_context(tc.tile_pool(name="attn", bufs=AHEAD + 4))
-        pair_pool = stack.enter_context(tc.tile_pool(name="pairs", bufs=8))
-        v_pool = stack.enter_context(tc.tile_pool(name="v", bufs=AHEAD // S_PAIR + 2))
-        flipped_pool = stack.enter_context(tc.tile_pool(name="flipped", bufs=2 * H))
+        attn_pool = stack.enter_context(tc.tile_pool(name="attn", bufs=UNITS * (AHEAD + 1)))
+        pair_pool = stack.enter_context(tc.tile_pool(name="pairs", bufs=UNITS))
+        v_pool = stack.enter_context(tc.tile_pool(name="v", bufs=AHEAD + 2))
+        flipped_pool = stack.enter_context(tc.tile_pool(name="flipped", bufs=2 * UNITS))
         ctx_pool = stack.enter_context(tc.tile_pool(name="ctx", bufs=3))
         grouped_pool = stack.enter_context(tc.tile_pool(name="grouped", bufs=3))
         code_pool = stack.enter_context(tc.tile_pool(name="codes", bufs=LAG + 2))
@@ -53,67 +55,84 @@ def tile_localtemporalattention_pa_kernel(tc, attn, v, W_out, out):
         ctx_codes = {}
         ctx_scales = {}
 
-        def load_attn(group, h):
-            b, s_half = divmod(group, S // S_GROUP)
-            rows = attn_pool.tile([P, J * P], BF16, name="attn_rows")
+        def place(group):
+            b, quarter = divmod(group, S // GROUP)
+            return b, slice(GROUP * quarter, GROUP * (quarter + 1))
+
+        def load_attn(group, unit):
+            b, locations = place(group)
+            rows = attn_pool.tile([P, UNIT, J * P], BF16, name="attn_rows")
             nc.sync.dma_start(
                 out=rows[:],
-                in_=attn[b, h, S_GROUP * s_half : S_GROUP * (s_half + 1)].rearrange(
-                    "s (th j) u -> (s th) (j u)", j=J
+                in_=attn[b, UNIT * unit : UNIT * (unit + 1), locations].rearrange(
+                    "h s (th j) u -> (s th) h (j u)", j=J
                 ),
             )
-            attn_rows[(group, h)] = rows
+            attn_rows[(group, unit)] = rows
 
-        def load_for(step):
-            if step >= STEPS:
-                return
-            if step % S_PAIR == 0:
-                b, s = divmod(step, S)
-                rows = v_pool.tile([P, S_PAIR, H, P], BF16, name="v_rows")
-                nc.sync.dma_start(out=rows[:], in_=v[b, :, s : s + S_PAIR])
-                v_rows[step // S_PAIR] = rows
-            group, h = divmod(step, S_GROUP)
-            if group + 1 < GROUPS:
-                load_attn(group + 1, h)
+        def load_v(group, pieces):
+            b, locations = place(group)
+            rows = v_pool.tile([P, GROUP, H, P], BF16, name="v_rows")
+            n = GROUP // pieces
+            for i in range(pieces):
+                part = slice(n * i, n * (i + 1))
+                nc.sync.dma_start(out=rows[:, part], in_=v[b, :, locations][:, part])
+            v_rows[group] = rows
 
-        def pair_frames(group, h):
-            pairs = pair_pool.tile([P, K, P, 2], BF16, name="pairs")
+        def pair_frames(group, unit):
+            pairs = pair_pool.tile([P, UNIT * K, P, 2], BF16, name="pairs")
             nc.vector.tensor_copy(
                 out=pairs[:],
-                in_=attn_rows[(group, h)][:].rearrange("p (k e u) -> p k u e", k=K, e=2),
+                in_=attn_rows[(group, unit)][:].rearrange("p h (k e u) -> p (h k) u e", k=K, e=2),
             )
-            attn_pairs[(group, h)] = pairs
+            attn_pairs[(group, unit)] = pairs
 
-        def flip(group, h, copy):
-            bank = psum.tile([P, K, P], F32, name="flip_bank", tag="bank")
-            words = attn_pairs[(group, h)][:].rearrange("p k u e -> p (k u e)").bitcast(F32)
-            for k in range(K):
-                nc.tensor.transpose(bank[:, k, :], words[:, P * k : P * (k + 1)], ident[:])
-            flipped = flipped_pool.tile([P, S_GROUP, P], BF16, name="flipped")
+        def flip(group, unit, copy):
+            bank = psum.tile([P, K, UNIT, P], F32, name="flip_bank", tag="bank")
+            words = attn_pairs[(group, unit)][:].rearrange("p k u e -> p (k u e)").bitcast(F32)
+            for h in range(UNIT):
+                for k in range(K):
+                    n = K * h + k
+                    nc.tensor.transpose(bank[:, k, h, :], words[:, P * n : P * (n + 1)], ident[:])
+            flipped = flipped_pool.tile([P, UNIT, GROUP, P], BF16, name="flipped")
             copy(
-                out=flipped[:].rearrange("u s t -> u (s t)").bitcast(F32).rearrange(
-                    "u (s th k) -> u s th k", s=S_GROUP, k=K
+                out=flipped[:].rearrange("u h s t -> u (h s t)").bitcast(F32).rearrange(
+                    "u (hs th k) -> u hs th k", th=TH, k=K
                 ),
-                in_=bank[:].rearrange("u k (s th) -> u s th k", s=S_GROUP),
+                in_=bank[:].rearrange("u k h (s th) -> u (h s) th k", s=GROUP),
             )
-            attn_t[(group, h)] = flipped
+            attn_t[(group, unit)] = flipped
 
-        def mix(step):
-            group, s_local = divmod(step, S_GROUP)
-            values = v_rows[step // S_PAIR]
+        def flip_plain(group, unit, copy):
+            bank = psum.tile([P, J, UNIT, P], BF16, name="flip_bank", tag="bank")
+            rows = attn_rows[(group, unit)]
+            for h in range(UNIT):
+                for j in range(J):
+                    nc.tensor.transpose(
+                        bank[:, j, h, :], rows[:, h, P * j : P * (j + 1)], ident_bf16[:]
+                    )
+            flipped = flipped_pool.tile([P, UNIT, GROUP, P], BF16, name="flipped")
+            copy(
+                out=flipped[:].rearrange("u h s (j th) -> u (h s) j th", j=J),
+                in_=bank[:].rearrange("u j h (s th) -> u (h s) j th", s=GROUP),
+            )
+            attn_t[(group, unit)] = flipped
+
+        def mix(step, copies=(nc.scalar.copy, nc.scalar.copy)):
+            group, s_local = divmod(step, GROUP)
             rows = ctx_pool.tile([P, PASSES, PACK // 2, P, 2], BF16, name="ctx_rows", align_bytes=64)
             for g in range(PASSES):
                 bank = psum.tile([P, HEADS, P], F32, name="ctx_bank", tag="bank")
                 for hh in range(HEADS):
-                    h = HEADS * g + hh
+                    unit, head = divmod(HEADS * g + hh, UNIT)
                     nc.tensor.matmul(
                         out=bank[:, hh, :],
-                        lhsT=attn_t[(group, h)][:, s_local, :],
-                        rhs=values[:, step % S_PAIR, h, :],
+                        lhsT=attn_t[(group, unit)][:, head, s_local, :],
+                        rhs=v_rows[group][:, s_local, HEADS * g + hh, :],
                         start=True,
                         stop=True,
                     )
-                nc.scalar.copy(
+                copies[g](
                     out=rows[:, g],
                     in_=bank[:].rearrange("t hh (q i e) -> t i (hh q) e", i=PACK // 2, e=2),
                 )
@@ -122,10 +141,11 @@ def tile_localtemporalattention_pa_kernel(tc, attn, v, W_out, out):
         def group_channels(step):
             words = ctx_rows[step][:].rearrange("t g i p e -> t (g i p e)").bitcast(F32)
             bank = psum.tile([P, PASSES, PACK // 2, P], F32, name="group_bank", tag="bank")
+            order = in_order if step < GROUP * PLAIN_GROUPS else ident
             for g in range(PASSES):
                 for i in range(PACK // 2):
-                    k = (PACK // 2) * g + i
-                    nc.tensor.transpose(bank[:, g, i, :], words[:, P * k : P * (k + 1)], ident[:])
+                    n = (PACK // 2) * g + i
+                    nc.tensor.transpose(bank[:, g, i, :], words[:, P * n : P * (n + 1)], order[:])
             grouped = grouped_pool.tile([P, PASSES * P * PACK], BF16, name="ctx_grouped", align_bytes=64)
             nc.vector.tensor_copy(
                 out=grouped[:].bitcast(F32).rearrange("p (g t i) -> p g t i", g=PASSES, i=PACK // 2),
@@ -159,61 +179,103 @@ def tile_localtemporalattention_pa_kernel(tc, attn, v, W_out, out):
                         start=(g == 0),
                         stop=(g == PASSES - 1),
                     )
-                nc.scalar.copy(out=result[:, cols], in_=bank[:])
+                copy = nc.vector.tensor_copy if (half == 1 and step % 2 == 1) else nc.scalar.copy
+                copy(out=result[:, cols], in_=bank[:])
             nc.sync.dma_start(out=out[b].rearrange("(t s) c -> s t c", s=S)[s], in_=result[:])
 
-        w_raw = []
-        for g in range(PASSES):
-            for hh in range(HEADS):
-                load_attn(0, HEADS * g + hh)
+        w_raw = {}
+        w_grouped = {}
+        w_codes = const.tile([P, PASSES, CO], U32, name="w_codes", align_bytes=64)
+        w_scales = const.tile([P, PASSES, CO], U8, name="w_scales", align_bytes=64)
+
+        def load_w(g):
             raw = const.tile([P, PACK, CO], BF16, name="w_raw%d" % g)
             nc.sync.dma_start(
                 out=raw[:],
                 in_=W_out[PACK * P * g : PACK * P * (g + 1), :].rearrange("(p i) n -> p i n", i=PACK),
             )
-            w_raw.append(raw)
+            w_raw[g] = raw
 
+        def group_w(g, half, copy):
+            cols = slice(BANK_COLS * half, BANK_COLS * (half + 1))
+            grouped = const.tile([P, BANK_COLS, PACK], BF16, name="w_grouped%d%d" % (g, half), align_bytes=64)
+            copy(
+                out=grouped[:].rearrange("p (c n) i -> p c i n", n=4),
+                in_=w_raw[g][:, :, cols].rearrange("p i (c n) -> p c i n", n=4),
+            )
+            w_grouped[(g, half)] = grouped
+
+        def quantise_w(g, half):
+            cols = slice(BANK_COLS * half, BANK_COLS * (half + 1))
+            nc.vector.quantize_mx(
+                out=w_codes[:, g, cols].bitcast(FP8X4),
+                scales=w_scales[:, g, cols],
+                in_=w_grouped[(g, half)][:].rearrange("p n i -> p (n i)"),
+            )
+
+        for unit in range(UNITS):
+            load_attn(0, unit)
+        load_v(0, 2)
+        for g in range(PASSES):
+            load_w(g)
+        for group in range(1, AHEAD):
+            for unit in range(UNITS):
+                load_attn(group, unit)
+            load_v(group, 1)
+
+        ident_bf16 = const.tile([P, P], BF16, name="ident_bf16")
+        masks.make_identity(nc, ident_bf16[:])
         ident = const.tile([P, P], F32, name="ident")
         masks.make_identity(nc, ident[:])
+        in_order = const.tile([P, P], F32, name="in_order")
+        nc.gpsimd.tensor_copy(
+            out=in_order[:].rearrange("x (th j) -> x th j", j=J),
+            in_=ident[:].rearrange("x (j th) -> x th j", j=J),
+        )
 
-        w_codes = const.tile([P, PASSES, CO], U32, name="w_codes", align_bytes=64)
-        w_scales = const.tile([P, PASSES, CO], U8, name="w_scales", align_bytes=64)
-        for g in range(PASSES):
-            for hh in range(HEADS):
-                pair_frames(0, HEADS * g + hh)
-            grouped = const.tile([P, CO, PACK], BF16, name="w_grouped%d" % g, align_bytes=64)
-            for half in range(COL_HALVES):
-                cols = slice(BANK_COLS * half, BANK_COLS * (half + 1))
-                nc.vector.tensor_copy(
-                    out=grouped[:, cols, :].rearrange("p (c n) i -> p c i n", n=4),
-                    in_=w_raw[g][:, :, cols].rearrange("p i (c n) -> p c i n", n=4),
-                )
-            for half in range(COL_HALVES):
-                cols = slice(BANK_COLS * half, BANK_COLS * (half + 1))
-                nc.vector.quantize_mx(
-                    out=w_codes[:, g, cols].bitcast(FP8X4),
-                    scales=w_scales[:, g, cols],
-                    in_=grouped[:, cols, :].rearrange("p n i -> p (n i)"),
-                )
+        both = (nc.scalar.copy, nc.vector.tensor_copy)
+        for unit in range(UNITS):
+            flip_plain(0, unit, both[unit % 2])
+        mix(0, both)
+        mix(1, both)
+        group_channels(0)
+        mix(2, both)
+        group_channels(1)
+        quantise_ctx(0)
+        mix(3, both)
+        group_channels(2)
+        quantise_ctx(1)
+        group_w(0, 0, nc.scalar.copy)
+        group_w(0, 1, nc.vector.tensor_copy)
+        group_channels(3)
+        quantise_ctx(2)
+        quantise_w(0, 0)
+        group_w(1, 0, nc.scalar.copy)
+        group_w(1, 1, nc.vector.tensor_copy)
+        quantise_w(0, 1)
+        quantise_w(1, 0)
+        quantise_w(1, 1)
+        for unit in range(UNITS):
+            flip_plain(1, unit, nc.scalar.copy)
+        quantise_ctx(3)
+        pair_frames(2, 0)
+        project(0)
+        project(1)
 
-        for h in range(H):
-            flip(0, h, nc.scalar.copy)
-
-        for step in range(AHEAD):
-            load_for(step)
-        pair_frames(1, 0)
-
-        for step in range(STEPS + LAG):
-            if step >= LAG:
-                quantise_ctx(step - LAG)
-            if step < STEPS:
-                load_for(step + AHEAD)
-                mix(step)
-                if step + S_GROUP < STEPS:
-                    flip(*divmod(step + S_GROUP, S_GROUP), nc.vector.tensor_copy)
-                if step + 1 + S_GROUP < STEPS:
-                    pair_frames(*divmod(step + 1 + S_GROUP, S_GROUP))
-            if 1 <= step <= STEPS:
+        for step in range(GROUP, STEPS + LAG):
+            group, unit = divmod(step, UNITS)
+            if group + AHEAD - 1 < GROUPS:
+                load_attn(group + AHEAD - 1, unit)
+                if unit == UNITS - 1:
+                    load_v(group + AHEAD - 1, 1)
+            if GROUP < step <= STEPS:
                 group_channels(step - 1)
-            if step >= LAG:
-                project(step - LAG)
+            if group + 1 < GROUPS:
+                flip(group + 1, unit, nc.vector.tensor_copy)
+            if step + UNITS + 1 < STEPS:
+                pair_frames(*divmod(step + UNITS + 1, UNITS))
+            if GROUP < step <= STEPS:
+                quantise_ctx(step - 1)
+            if step < STEPS:
+                mix(step)
+            project(step - LAG)

@@ -16,17 +16,14 @@ PASSES = 2
 HEADS = H // PASSES
 BANK_COLS = 512
 COL_HALVES = CO // BANK_COLS
-GROUP = 4
-TH = P // GROUP
-J = P // TH
-K = J // 2
-UNIT = 2
-UNITS = H // UNIT
+WINDOW = 5
+FOLD = 16
+M = P // FOLD
+UNIT = 8
+V_STEPS = 4
 STEPS = B * S
-GROUPS = STEPS // GROUP
+GROUPS = ((0, 4), (4, 4), (8, 8), (16, 8), (24, 8))
 LAG = 2
-PLAIN_GROUPS = 2
-AHEAD = 3
 
 FLOPS = 2 * B * H * S * P * P * P + 2 * B * S * P * H * P * CO
 
@@ -36,10 +33,10 @@ def tile_localtemporalattention_pa_kernel(tc, attn, v, W_out, out):
     with ExitStack() as stack:
         stack.enter_context(tc.manual_schedule())
         const = stack.enter_context(tc.tile_pool(name="const", bufs=1))
-        attn_pool = stack.enter_context(tc.tile_pool(name="attn", bufs=UNITS * (AHEAD + 1)))
-        pair_pool = stack.enter_context(tc.tile_pool(name="pairs", bufs=UNITS))
-        v_pool = stack.enter_context(tc.tile_pool(name="v", bufs=AHEAD + 2))
-        flipped_pool = stack.enter_context(tc.tile_pool(name="flipped", bufs=2 * UNITS))
+        attn_pool = stack.enter_context(tc.tile_pool(name="attn", bufs=20))
+        folded_pool = stack.enter_context(tc.tile_pool(name="folded", bufs=6))
+        v_pool = stack.enter_context(tc.tile_pool(name="v", bufs=6))
+        attn_t_pool = stack.enter_context(tc.tile_pool(name="attn_t", bufs=16))
         ctx_pool = stack.enter_context(tc.tile_pool(name="ctx", bufs=3))
         grouped_pool = stack.enter_context(tc.tile_pool(name="grouped", bufs=3))
         code_pool = stack.enter_context(tc.tile_pool(name="codes", bufs=LAG + 2))
@@ -48,91 +45,89 @@ def tile_localtemporalattention_pa_kernel(tc, attn, v, W_out, out):
 
         attn_rows = {}
         v_rows = {}
-        attn_pairs = {}
+        folded = {}
         attn_t = {}
         ctx_rows = {}
         ctx_grouped = {}
         ctx_codes = {}
         ctx_scales = {}
 
-        def place(group):
-            b, quarter = divmod(group, S // GROUP)
-            return b, slice(GROUP * quarter, GROUP * (quarter + 1))
+        def group_of(step):
+            return [g for g in GROUPS if g[0] <= step < g[0] + g[1]][0]
 
-        def load_attn(group, unit):
-            b, locations = place(group)
-            rows = attn_pool.tile([P, UNIT, J * P], BF16, name="attn_rows")
+        def load_attn(unit):
+            first, n = group_of(unit)
+            b, s = divmod(first, S)
+            heads = UNIT // n
+            h = heads * (unit - first)
+            rows = attn_pool.tile([P, UNIT * P], BF16, name="attn_rows")
             nc.sync.dma_start(
-                out=rows[:],
-                in_=attn[b, UNIT * unit : UNIT * (unit + 1), locations].rearrange(
-                    "h s (th j) u -> (s th) h (j u)", j=J
-                ),
+                out=rows[:].rearrange("p (h x) -> p h x", h=heads),
+                in_=attn[b, h : h + heads, s : s + n].rearrange("h s (th j) u -> (s th) h (j u)", j=n),
             )
-            attn_rows[(group, unit)] = rows
+            attn_rows[unit] = rows
 
-        def load_v(group, pieces):
-            b, locations = place(group)
-            rows = v_pool.tile([P, GROUP, H, P], BF16, name="v_rows")
-            n = GROUP // pieces
+        def load_v(tile_number, pieces=1):
+            b, s = divmod(V_STEPS * tile_number, S)
+            rows = v_pool.tile([P, V_STEPS, H, P], BF16, name="v_rows")
+            n = V_STEPS // pieces
             for i in range(pieces):
-                part = slice(n * i, n * (i + 1))
-                nc.sync.dma_start(out=rows[:, part], in_=v[b, :, locations][:, part])
-            v_rows[group] = rows
+                nc.sync.dma_start(
+                    out=rows[:, n * i : n * (i + 1)], in_=v[b, :, s + n * i : s + n * (i + 1)]
+                )
+            v_rows[tile_number] = rows
 
-        def pair_frames(group, unit):
-            pairs = pair_pool.tile([P, UNIT * K, P, 2], BF16, name="pairs")
-            nc.vector.tensor_copy(
-                out=pairs[:],
-                in_=attn_rows[(group, unit)][:].rearrange("p h (k e u) -> p (h k) u e", k=K, e=2),
-            )
-            attn_pairs[(group, unit)] = pairs
-
-        def flip(group, unit, copy):
-            bank = psum.tile([P, K, UNIT, P], F32, name="flip_bank", tag="bank")
-            words = attn_pairs[(group, unit)][:].rearrange("p k u e -> p (k u e)").bitcast(F32)
-            for h in range(UNIT):
-                for k in range(K):
-                    n = K * h + k
-                    nc.tensor.transpose(bank[:, k, h, :], words[:, P * n : P * (n + 1)], ident[:])
-            flipped = flipped_pool.tile([P, UNIT, GROUP, P], BF16, name="flipped")
-            copy(
-                out=flipped[:].rearrange("u h s t -> u (h s t)").bitcast(F32).rearrange(
-                    "u (hs th k) -> u hs th k", th=TH, k=K
-                ),
-                in_=bank[:].rearrange("u k h (s th) -> u (h s) th k", s=GROUP),
-            )
-            attn_t[(group, unit)] = flipped
-
-        def flip_plain(group, unit, copy):
-            bank = psum.tile([P, J, UNIT, P], BF16, name="flip_bank", tag="bank")
-            rows = attn_rows[(group, unit)]
-            for h in range(UNIT):
-                for j in range(J):
-                    nc.tensor.transpose(
-                        bank[:, j, h, :], rows[:, h, P * j : P * (j + 1)], ident_bf16[:]
+        def fold(unit):
+            first, n = group_of(unit)
+            heads = UNIT // n
+            bank = psum.tile([P, n, UNIT * FOLD // n], F32, name="fold_bank", tag="bank")
+            width = n * FOLD // n
+            for h in range(heads):
+                for j in range(n):
+                    k = n * h + j
+                    nc.tensor.matmul(
+                        out=bank[:, j, width * h : width * (h + 1)],
+                        lhsT=attn_rows[unit][:, P * k : P * (k + 1)],
+                        rhs=fold_matrix[n][:],
+                        start=True,
+                        stop=True,
                     )
-            flipped = flipped_pool.tile([P, UNIT, GROUP, P], BF16, name="flipped")
-            copy(
-                out=flipped[:].rearrange("u h s (j th) -> u (h s) j th", j=J),
-                in_=bank[:].rearrange("u j h (s th) -> u (h s) j th", s=GROUP),
+            columns = folded_pool.tile([P, UNIT, FOLD], BF16, name="folded")
+            nc.scalar.copy(
+                out=columns[:].rearrange("u hs (a j) -> u hs a j", j=n),
+                in_=bank[:].rearrange("u j (hs a) -> u hs a j", hs=UNIT),
             )
-            attn_t[(group, unit)] = flipped
+            folded[unit] = columns
 
-        def mix(step, copies=(nc.scalar.copy, nc.scalar.copy)):
-            group, s_local = divmod(step, GROUP)
+        def unfold(unit):
+            full = attn_t_pool.tile([P, UNIT, M, FOLD], BF16, name="attn_t")
+            nc.vector.tensor_tensor(
+                out=full[:],
+                in0=folded[unit][:].unsqueeze(2).to_broadcast([P, UNIT, M, FOLD]),
+                in1=band[:].rearrange("u (m r) -> u m r", r=FOLD).unsqueeze(1).to_broadcast(
+                    [P, UNIT, M, FOLD]
+                ),
+                op=mybir.AluOpType.mult,
+            )
+            attn_t[unit] = full
+
+        def mix(step):
+            first, n = group_of(step)
             rows = ctx_pool.tile([P, PASSES, PACK // 2, P, 2], BF16, name="ctx_rows", align_bytes=64)
             for g in range(PASSES):
                 bank = psum.tile([P, HEADS, P], F32, name="ctx_bank", tag="bank")
                 for hh in range(HEADS):
-                    unit, head = divmod(HEADS * g + hh, UNIT)
+                    h = HEADS * g + hh
+                    unit, h_local = divmod(h, UNIT // n)
                     nc.tensor.matmul(
                         out=bank[:, hh, :],
-                        lhsT=attn_t[(group, unit)][:, head, s_local, :],
-                        rhs=v_rows[group][:, s_local, HEADS * g + hh, :],
+                        lhsT=attn_t[first + unit][:, n * h_local + step - first].rearrange("u m r -> u (m r)"),
+                        rhs=v_rows[step // V_STEPS][:, step % V_STEPS, h, :],
                         start=True,
                         stop=True,
                     )
-                copies[g](
+                copy = (nc.scalar.copy, nc.vector.tensor_copy)[g]
+                copy(
                     out=rows[:, g],
                     in_=bank[:].rearrange("t hh (q i e) -> t i (hh q) e", i=PACK // 2, e=2),
                 )
@@ -141,11 +136,10 @@ def tile_localtemporalattention_pa_kernel(tc, attn, v, W_out, out):
         def group_channels(step):
             words = ctx_rows[step][:].rearrange("t g i p e -> t (g i p e)").bitcast(F32)
             bank = psum.tile([P, PASSES, PACK // 2, P], F32, name="group_bank", tag="bank")
-            order = in_order if step < GROUP * PLAIN_GROUPS else ident
             for g in range(PASSES):
                 for i in range(PACK // 2):
                     n = (PACK // 2) * g + i
-                    nc.tensor.transpose(bank[:, g, i, :], words[:, P * n : P * (n + 1)], order[:])
+                    nc.tensor.transpose(bank[:, g, i, :], words[:, P * n : P * (n + 1)], ident[:])
             grouped = grouped_pool.tile([P, PASSES * P * PACK], BF16, name="ctx_grouped", align_bytes=64)
             nc.vector.tensor_copy(
                 out=grouped[:].bitcast(F32).rearrange("p (g t i) -> p g t i", g=PASSES, i=PACK // 2),
@@ -179,8 +173,7 @@ def tile_localtemporalattention_pa_kernel(tc, attn, v, W_out, out):
                         start=(g == 0),
                         stop=(g == PASSES - 1),
                     )
-                copy = nc.vector.tensor_copy if (half == 1 and step % 2 == 1) else nc.scalar.copy
-                copy(out=result[:, cols], in_=bank[:])
+                nc.scalar.copy(out=result[:, cols], in_=bank[:])
             nc.sync.dma_start(out=out[b].rearrange("(t s) c -> s t c", s=S)[s], in_=result[:])
 
         w_raw = {}
@@ -213,69 +206,96 @@ def tile_localtemporalattention_pa_kernel(tc, attn, v, W_out, out):
                 in_=w_grouped[(g, half)][:].rearrange("p n i -> p (n i)"),
             )
 
-        for unit in range(UNITS):
-            load_attn(0, unit)
-        load_v(0, 2)
+        for unit in range(4):
+            load_attn(unit)
+        load_v(0, pieces=2)
         for g in range(PASSES):
             load_w(g)
-        for group in range(1, AHEAD):
-            for unit in range(UNITS):
-                load_attn(group, unit)
-            load_v(group, 1)
+        for unit in range(4, 8):
+            load_attn(unit)
+        load_v(1)
+        for unit in range(8, 16):
+            load_attn(unit)
+        load_v(2)
+        later = []
+        for tile_number in range(3, STEPS // V_STEPS):
+            for unit in range(V_STEPS * (tile_number + 1), min(STEPS, V_STEPS * (tile_number + 2))):
+                later.append((load_attn, unit))
+            later.append((load_v, tile_number))
 
-        ident_bf16 = const.tile([P, P], BF16, name="ident_bf16")
-        masks.make_identity(nc, ident_bf16[:])
         ident = const.tile([P, P], F32, name="ident")
         masks.make_identity(nc, ident[:])
-        in_order = const.tile([P, P], F32, name="in_order")
-        nc.gpsimd.tensor_copy(
-            out=in_order[:].rearrange("x (th j) -> x th j", j=J),
-            in_=ident[:].rearrange("x (j th) -> x th j", j=J),
-        )
+        fold_matrix = {}
+        for n in (4, 8):
+            sums = const.tile([P, FOLD], F32, name="fold_sums%d" % n)
+            matrix = const.tile([P, FOLD], BF16, name="fold%d" % n)
+            nc.vector.tensor_reduce(
+                out=sums[:].rearrange("p (s a) -> p s a", s=n),
+                in_=ident[:].rearrange("p (s q a) -> p s a q", s=n, a=FOLD // n),
+                axis=mybir.AxisListType.X,
+                op=mybir.AluOpType.add,
+            )
+            nc.vector.tensor_copy(out=matrix[:], in_=sums[:])
+            fold_matrix[n] = matrix
+        band = const.tile([P, P], BF16, name="band")
+        nc.gpsimd.memset(band[:], 1.0)
+        for sign in (1, -1):
+            nc.gpsimd.affine_select(
+                out=band[:],
+                in_=band[:],
+                pattern=[[-sign, P]],
+                compare_op=mybir.AluOpType.is_ge,
+                fill=0.0,
+                base=WINDOW,
+                channel_multiplier=sign,
+            )
 
-        both = (nc.scalar.copy, nc.vector.tensor_copy)
-        for unit in range(UNITS):
-            flip_plain(0, unit, both[unit % 2])
-        mix(0, both)
-        mix(1, both)
+        for unit in range(4):
+            fold(unit)
+            unfold(unit)
+        mix(0)
+        mix(1)
         group_channels(0)
-        mix(2, both)
+        mix(2)
         group_channels(1)
         quantise_ctx(0)
-        mix(3, both)
+        mix(3)
         group_channels(2)
         quantise_ctx(1)
-        group_w(0, 0, nc.scalar.copy)
-        group_w(0, 1, nc.vector.tensor_copy)
+        group_w(0, 0, nc.vector.tensor_copy)
+        group_w(0, 1, nc.scalar.copy)
         group_channels(3)
         quantise_ctx(2)
         quantise_w(0, 0)
-        group_w(1, 0, nc.scalar.copy)
-        group_w(1, 1, nc.vector.tensor_copy)
+        group_w(1, 0, nc.vector.tensor_copy)
+        group_w(1, 1, nc.scalar.copy)
         quantise_w(0, 1)
+        quantise_ctx(3)
         quantise_w(1, 0)
         quantise_w(1, 1)
-        for unit in range(UNITS):
-            flip_plain(1, unit, nc.scalar.copy)
-        quantise_ctx(3)
-        pair_frames(2, 0)
+        for unit in range(4, 8):
+            fold(unit)
+            unfold(unit)
         project(0)
         project(1)
 
-        for step in range(GROUP, STEPS + LAG):
-            group, unit = divmod(step, UNITS)
-            if group + AHEAD - 1 < GROUPS:
-                load_attn(group + AHEAD - 1, unit)
-                if unit == UNITS - 1:
-                    load_v(group + AHEAD - 1, 1)
-            if GROUP < step <= STEPS:
+        for step in range(4, STEPS + LAG):
+            for load, number in later[:2]:
+                load(number)
+            later = later[2:]
+            if 4 < step <= STEPS:
                 group_channels(step - 1)
-            if group + 1 < GROUPS:
-                flip(group + 1, unit, nc.vector.tensor_copy)
-            if step + UNITS + 1 < STEPS:
-                pair_frames(*divmod(step + UNITS + 1, UNITS))
-            if GROUP < step <= STEPS:
-                quantise_ctx(step - 1)
+            units = ()
+            if step < GROUPS[-1][0]:
+                first, n = group_of(step)
+                ratio = group_of(first + n)[1] // n
+                units = range(first + n + ratio * (step - first), first + n + ratio * (step - first + 1))
+            for unit in units:
+                fold(unit)
             if step < STEPS:
                 mix(step)
+            for unit in units:
+                unfold(unit)
+            if 4 < step <= STEPS:
+                quantise_ctx(step - 1)
             project(step - LAG)

@@ -111,10 +111,12 @@ def tile_localtemporalattention_pa_kernel(tc, attn, v, W_out, out):
             )
             attn_t[unit] = full
 
-        def mix(step):
+        def mix(step, passes=range(PASSES)):
             first, n = group_of(step)
-            rows = ctx_pool.tile([P, PASSES, PACK // 2, P, 2], BF16, name="ctx_rows", align_bytes=64)
-            for g in range(PASSES):
+            if step not in ctx_rows:
+                rows = ctx_pool.tile([P, PASSES, PACK // 2, P, 2], BF16, name="ctx_rows", align_bytes=64)
+                ctx_rows[step] = rows
+            for g in passes:
                 bank = psum.tile([P, HEADS, P], F32, name="ctx_bank", tag="bank")
                 for hh in range(HEADS):
                     h = HEADS * g + hh
@@ -128,10 +130,9 @@ def tile_localtemporalattention_pa_kernel(tc, attn, v, W_out, out):
                     )
                 copy = (nc.scalar.copy, nc.vector.tensor_copy)[g]
                 copy(
-                    out=rows[:, g],
+                    out=ctx_rows[step][:, g],
                     in_=bank[:].rearrange("t hh (q i e) -> t i (hh q) e", i=PACK // 2, e=2),
                 )
-            ctx_rows[step] = rows
 
         def group_channels(step):
             words = ctx_rows[step][:].rearrange("t g i p e -> t (g i p e)").bitcast(F32)
@@ -283,8 +284,12 @@ def tile_localtemporalattention_pa_kernel(tc, attn, v, W_out, out):
             for load, number in later[:2]:
                 load(number)
             later = later[2:]
+            if step < STEPS:
+                mix(step, (0,))
             if 4 < step <= STEPS:
                 group_channels(step - 1)
+            if step < STEPS:
+                mix(step, (1,))
             units = ()
             if step < GROUPS[-1][0]:
                 first, n = group_of(step)
@@ -292,9 +297,6 @@ def tile_localtemporalattention_pa_kernel(tc, attn, v, W_out, out):
                 units = range(first + n + ratio * (step - first), first + n + ratio * (step - first + 1))
             for unit in units:
                 fold(unit)
-            if step < STEPS:
-                mix(step)
-            for unit in units:
                 unfold(unit)
             if 4 < step <= STEPS:
                 quantise_ctx(step - 1)

@@ -40,7 +40,7 @@ def tile_localtemporalattention_pa_kernel(tc, attn, v, W_out, out):
         ctx_pool = stack.enter_context(tc.tile_pool(name="ctx", bufs=3))
         grouped_pool = stack.enter_context(tc.tile_pool(name="grouped", bufs=3))
         code_pool = stack.enter_context(tc.tile_pool(name="codes", bufs=LAG + 2))
-        out_pool = stack.enter_context(tc.tile_pool(name="out", bufs=6))
+        out_pool = stack.enter_context(tc.tile_pool(name="out", bufs=4))
         psum = stack.enter_context(tc.psum_pool(name="psum", bufs=8))
 
         attn_rows = {}
@@ -51,6 +51,7 @@ def tile_localtemporalattention_pa_kernel(tc, attn, v, W_out, out):
         ctx_grouped = {}
         ctx_codes = {}
         ctx_scales = {}
+        results = {}
 
         def group_of(step):
             return [g for g in GROUPS if g[0] <= step < g[0] + g[1]][0]
@@ -159,7 +160,11 @@ def tile_localtemporalattention_pa_kernel(tc, attn, v, W_out, out):
 
         def project(step):
             b, s = divmod(step, S)
-            result = out_pool.tile([P, CO], F32, name="result")
+            pair, last = step // 2, step >= STEPS - 2
+            if pair not in results:
+                results[pair] = out_pool.tile([P, 2, CO], F32, name="result")
+            result = results[pair]
+            rows_out = out[b].rearrange("(t s) c -> t s c", s=S)
             for half in range(COL_HALVES):
                 cols = slice(BANK_COLS * half, BANK_COLS * (half + 1))
                 bank = psum.tile([P, BANK_COLS], F32, name="out_bank", tag="bank")
@@ -174,8 +179,12 @@ def tile_localtemporalattention_pa_kernel(tc, attn, v, W_out, out):
                         start=(g == 0),
                         stop=(g == PASSES - 1),
                     )
-                nc.scalar.copy(out=result[:, cols], in_=bank[:])
-            nc.sync.dma_start(out=out[b].rearrange("(t s) c -> s t c", s=S)[s], in_=result[:])
+                copy = nc.vector.tensor_copy if half == 1 and step >= GROUPS[-1][0] - LAG else nc.scalar.copy
+                copy(out=result[:, step % 2, cols], in_=bank[:])
+                if last:
+                    nc.sync.dma_start(out=rows_out[:, s, cols], in_=result[:, step % 2, cols])
+            if step % 2 == 1 and not last:
+                nc.sync.dma_start(out=rows_out[:, s - 1 : s + 1], in_=result[:])
 
         w_raw = {}
         w_grouped = {}
@@ -207,11 +216,11 @@ def tile_localtemporalattention_pa_kernel(tc, attn, v, W_out, out):
                 in_=w_grouped[(g, half)][:].rearrange("p n i -> p (n i)"),
             )
 
+        load_w(0)
         for unit in range(4):
             load_attn(unit)
         load_v(0, pieces=2)
-        for g in range(PASSES):
-            load_w(g)
+        load_w(1)
         for unit in range(4, 8):
             load_attn(unit)
         load_v(1)
@@ -251,32 +260,30 @@ def tile_localtemporalattention_pa_kernel(tc, attn, v, W_out, out):
                 channel_multiplier=sign,
             )
 
+        group_w(0, 0, nc.vector.tensor_copy)
         for unit in range(4):
             fold(unit)
             unfold(unit)
+        group_w(0, 1, nc.scalar.copy)
+        quantise_w(0, 0)
         mix(0)
         mix(1)
         group_channels(0)
         mix(2)
-        group_channels(1)
         quantise_ctx(0)
         mix(3)
-        group_channels(2)
-        quantise_ctx(1)
-        group_w(0, 0, nc.vector.tensor_copy)
-        group_w(0, 1, nc.scalar.copy)
-        group_channels(3)
-        quantise_ctx(2)
-        quantise_w(0, 0)
         group_w(1, 0, nc.vector.tensor_copy)
         group_w(1, 1, nc.scalar.copy)
-        quantise_w(0, 1)
-        quantise_ctx(3)
+        group_channels(1)
         quantise_w(1, 0)
+        quantise_w(0, 1)
+        quantise_ctx(1)
         quantise_w(1, 1)
+        group_channels(2)
         for unit in range(4, 8):
             fold(unit)
             unfold(unit)
+        quantise_ctx(2)
         project(0)
         project(1)
 
@@ -286,7 +293,7 @@ def tile_localtemporalattention_pa_kernel(tc, attn, v, W_out, out):
             later = later[2:]
             if step < STEPS:
                 mix(step, (0,))
-            if 4 < step <= STEPS:
+            if step <= STEPS:
                 group_channels(step - 1)
             if step < STEPS:
                 mix(step, (1,))
@@ -298,6 +305,6 @@ def tile_localtemporalattention_pa_kernel(tc, attn, v, W_out, out):
             for unit in units:
                 fold(unit)
                 unfold(unit)
-            if 4 < step <= STEPS:
+            if step <= STEPS:
                 quantise_ctx(step - 1)
             project(step - LAG)

from contextlib import ExitStack

import concourse.masks as masks
import concourse.mybir as mybir

BF16 = mybir.dt.bfloat16
F32 = mybir.dt.float32
U32 = mybir.dt.uint32
U8 = mybir.dt.uint8
FP8X4 = mybir.dt.float8_e4m3fn_x4

P = 128
B, S, H, CO = 2, 16, 8, 1024
PACK = 4
PASSES = 2
HEADS = H // PASSES
BANK_COLS = 512
COL_HALVES = CO // BANK_COLS
WINDOW = 5
FOLD = 16
M = P // FOLD
UNIT = 8
V_STEPS = 4
STEPS = B * S
GROUPS = ((0, 4), (4, 4), (8, 8), (16, 8), (24, 8))
LAG = 2

FLOPS = 2 * B * H * S * P * P * P + 2 * B * S * P * H * P * CO


def tile_localtemporalattention_pa_kernel(tc, attn, v, W_out, out):
    nc = tc.nc
    with ExitStack() as stack:
        stack.enter_context(tc.manual_schedule())
        const = stack.enter_context(tc.tile_pool(name="const", bufs=1))
        attn_pool = stack.enter_context(tc.tile_pool(name="attn", bufs=20))
        folded_pool = stack.enter_context(tc.tile_pool(name="folded", bufs=6))
        v_pool = stack.enter_context(tc.tile_pool(name="v", bufs=6))
        attn_t_pool = stack.enter_context(tc.tile_pool(name="attn_t", bufs=16))
        ctx_pool = stack.enter_context(tc.tile_pool(name="ctx", bufs=3))
        grouped_pool = stack.enter_context(tc.tile_pool(name="grouped", bufs=3))
        code_pool = stack.enter_context(tc.tile_pool(name="codes", bufs=LAG + 2))
        out_pool = stack.enter_context(tc.tile_pool(name="out", bufs=4))
        psum = stack.enter_context(tc.psum_pool(name="psum", bufs=8))

        attn_rows = {}
        v_rows = {}
        folded = {}
        attn_t = {}
        ctx_rows = {}
        ctx_grouped = {}
        ctx_codes = {}
        ctx_scales = {}
        results = {}

        def group_of(step):
            return [g for g in GROUPS if g[0] <= step < g[0] + g[1]][0]

        def load_attn(unit):
            first, n = group_of(unit)
            b, s = divmod(first, S)
            heads = UNIT // n
            h = heads * (unit - first)
            rows = attn_pool.tile([P, UNIT * P], BF16, name="attn_rows")
            nc.sync.dma_start(
                out=rows[:].rearrange("p (h x) -> p h x", h=heads),
                in_=attn[b, h : h + heads, s : s + n].rearrange("h s (th j) u -> (s th) h (j u)", j=n),
            )
            attn_rows[unit] = rows

        def load_v(tile_number, pieces=1):
            b, s = divmod(V_STEPS * tile_number, S)
            rows = v_pool.tile([P, V_STEPS, H, P], BF16, name="v_rows")
            n = V_STEPS // pieces
            for i in range(pieces):
                nc.sync.dma_start(
                    out=rows[:, n * i : n * (i + 1)], in_=v[b, :, s + n * i : s + n * (i + 1)]
                )
            v_rows[tile_number] = rows

        def fold(unit):
            first, n = group_of(unit)
            heads = UNIT // n
            bank = psum.tile([P, n, UNIT * FOLD // n], F32, name="fold_bank", tag="bank")
            width = n * FOLD // n
            for h in range(heads):
                for j in range(n):
                    k = n * h + j
                    nc.tensor.matmul(
                        out=bank[:, j, width * h : width * (h + 1)],
                        lhsT=attn_rows[unit][:, P * k : P * (k + 1)],
                        rhs=fold_matrix[n][:],
                        start=True,
                        stop=True,
                    )
            columns = folded_pool.tile([P, UNIT, FOLD], BF16, name="folded")
            nc.scalar.copy(
                out=columns[:].rearrange("u hs (a j) -> u hs a j", j=n),
                in_=bank[:].rearrange("u j (hs a) -> u hs a j", hs=UNIT),
            )
            folded[unit] = columns

        def unfold(unit):
            full = attn_t_pool.tile([P, UNIT, M, FOLD], BF16, name="attn_t")
            nc.vector.tensor_tensor(
                out=full[:],
                in0=folded[unit][:].unsqueeze(2).to_broadcast([P, UNIT, M, FOLD]),
                in1=band[:].rearrange("u (m r) -> u m r", r=FOLD).unsqueeze(1).to_broadcast(
                    [P, UNIT, M, FOLD]
                ),
                op=mybir.AluOpType.mult,
            )
            attn_t[unit] = full

        def mix(step, passes=range(PASSES)):
            first, n = group_of(step)
            if step not in ctx_rows:
                rows = ctx_pool.tile([P, PASSES, PACK // 2, P, 2], BF16, name="ctx_rows", align_bytes=64)
                ctx_rows[step] = rows
            for g in passes:
                bank = psum.tile([P, HEADS, P], F32, name="ctx_bank", tag="bank")
                for hh in range(HEADS):
                    h = HEADS * g + hh
                    unit, h_local = divmod(h, UNIT // n)
                    nc.tensor.matmul(
                        out=bank[:, hh, :],
                        lhsT=attn_t[first + unit][:, n * h_local + step - first].rearrange("u m r -> u (m r)"),
                        rhs=v_rows[step // V_STEPS][:, step % V_STEPS, h, :],
                        start=True,
                        stop=True,
                    )
                copy = (nc.scalar.copy, nc.vector.tensor_copy)[g]
                copy(
                    out=ctx_rows[step][:, g],
                    in_=bank[:].rearrange("t hh (q i e) -> t i (hh q) e", i=PACK // 2, e=2),
                )

        def group_channels(step):
            words = ctx_rows[step][:].rearrange("t g i p e -> t (g i p e)").bitcast(F32)
            bank = psum.tile([P, PASSES, PACK // 2, P], F32, name="group_bank", tag="bank")
            for g in range(PASSES):
                for i in range(PACK // 2):
                    n = (PACK // 2) * g + i
                    nc.tensor.transpose(bank[:, g, i, :], words[:, P * n : P * (n + 1)], ident[:])
            grouped = grouped_pool.tile([P, PASSES * P * PACK], BF16, name="ctx_grouped", align_bytes=64)
            nc.vector.tensor_copy(
                out=grouped[:].bitcast(F32).rearrange("p (g t i) -> p g t i", g=PASSES, i=PACK // 2),
                in_=bank[:].rearrange("p g i t -> p g t i"),
            )
            ctx_grouped[step] = grouped

        def quantise_ctx(step):
            codes = code_pool.tile([P, PASSES * P], U32, name="ctx_codes", align_bytes=64)
            scales = code_pool.tile([P, PASSES * P], U8, name="ctx_scales", align_bytes=64)
            nc.vector.quantize_mx(
                out=codes[:].bitcast(FP8X4), scales=scales[:], in_=ctx_grouped[step][:]
            )
            ctx_codes[step] = codes
            ctx_scales[step] = scales

        def project(step):
            b, s = divmod(step, S)
            pair, last = step // 2, step >= STEPS - 2
            if pair not in results:
                results[pair] = out_pool.tile([P, 2, CO], F32, name="result")
            result = results[pair]
            rows_out = out[b].rearrange("(t s) c -> t s c", s=S)
            for half in range(COL_HALVES):
                cols = slice(BANK_COLS * half, BANK_COLS * (half + 1))
                bank = psum.tile([P, BANK_COLS], F32, name="out_bank", tag="bank")
                for g in range(PASSES):
                    rows = slice(P * g, P * (g + 1))
                    nc.tensor.matmul_mx(
                        out=bank[:],
                        lhsT=ctx_codes[step][:, rows].bitcast(FP8X4),
                        lhsT_scale=ctx_scales[step][:, rows],
                        rhs=w_codes[:, g, cols].bitcast(FP8X4),
                        rhs_scale=w_scales[:, g, cols],
                        start=(g == 0),
                        stop=(g == PASSES - 1),
                    )
                copy = nc.vector.tensor_copy if half == 1 and step >= GROUPS[-1][0] - LAG else nc.scalar.copy
                copy(out=result[:, step % 2, cols], in_=bank[:])
                if last:
                    nc.sync.dma_start(out=rows_out[:, s, cols], in_=result[:, step % 2, cols])
            if step % 2 == 1 and not last:
                nc.sync.dma_start(out=rows_out[:, s - 1 : s + 1], in_=result[:])

        w_raw = {}
        w_grouped = {}
        w_codes = const.tile([P, PASSES, CO], U32, name="w_codes", align_bytes=64)
        w_scales = const.tile([P, PASSES, CO], U8, name="w_scales", align_bytes=64)

        def load_w(g):
            raw = const.tile([P, PACK, CO], BF16, name="w_raw%d" % g)
            nc.sync.dma_start(
                out=raw[:],
                in_=W_out[PACK * P * g : PACK * P * (g + 1), :].rearrange("(p i) n -> p i n", i=PACK),
            )
            w_raw[g] = raw

        def group_w(g, half, copy):
            cols = slice(BANK_COLS * half, BANK_COLS * (half + 1))
            grouped = const.tile([P, BANK_COLS, PACK], BF16, name="w_grouped%d%d" % (g, half), align_bytes=64)
            copy(
                out=grouped[:].rearrange("p (c n) i -> p c i n", n=4),
                in_=w_raw[g][:, :, cols].rearrange("p i (c n) -> p c i n", n=4),
            )
            w_grouped[(g, half)] = grouped

        def quantise_w(g, half):
            cols = slice(BANK_COLS * half, BANK_COLS * (half + 1))
            nc.vector.quantize_mx(
                out=w_codes[:, g, cols].bitcast(FP8X4),
                scales=w_scales[:, g, cols],
                in_=w_grouped[(g, half)][:].rearrange("p n i -> p (n i)"),
            )

        load_w(0)
        for unit in range(4):
            load_attn(unit)
        load_v(0, pieces=2)
        load_w(1)
        for unit in range(4, 8):
            load_attn(unit)
        load_v(1)
        for unit in range(8, 16):
            load_attn(unit)
        load_v(2)
        later = []
        for tile_number in range(3, STEPS // V_STEPS):
            for unit in range(V_STEPS * (tile_number + 1), min(STEPS, V_STEPS * (tile_number + 2))):
                later.append((load_attn, unit))
            later.append((load_v, tile_number))

        ident = const.tile([P, P], F32, name="ident")
        masks.make_identity(nc, ident[:])
        fold_matrix = {}
        for n in (4, 8):
            sums = const.tile([P, FOLD], F32, name="fold_sums%d" % n)
            matrix = const.tile([P, FOLD], BF16, name="fold%d" % n)
            nc.vector.tensor_reduce(
                out=sums[:].rearrange("p (s a) -> p s a", s=n),
                in_=ident[:].rearrange("p (s q a) -> p s a q", s=n, a=FOLD // n),
                axis=mybir.AxisListType.X,
                op=mybir.AluOpType.add,
            )
            nc.vector.tensor_copy(out=matrix[:], in_=sums[:])
            fold_matrix[n] = matrix
        band = const.tile([P, P], BF16, name="band")
        nc.gpsimd.memset(band[:], 1.0)
        for sign in (1, -1):
            nc.gpsimd.affine_select(
                out=band[:],
                in_=band[:],
                pattern=[[-sign, P]],
                compare_op=mybir.AluOpType.is_ge,
                fill=0.0,
                base=WINDOW,
                channel_multiplier=sign,
            )

        group_w(0, 0, nc.vector.tensor_copy)
        for unit in range(4):
            fold(unit)
            unfold(unit)
        group_w(0, 1, nc.scalar.copy)
        quantise_w(0, 0)
        mix(0)
        mix(1)
        group_channels(0)
        mix(2)
        quantise_ctx(0)
        mix(3)
        group_w(1, 0, nc.vector.tensor_copy)
        group_w(1, 1, nc.scalar.copy)
        group_channels(1)
        quantise_w(1, 0)
        quantise_w(0, 1)
        quantise_ctx(1)
        quantise_w(1, 1)
        group_channels(2)
        for unit in range(4, 8):
            fold(unit)
            unfold(unit)
        quantise_ctx(2)
        project(0)
        project(1)

        for step in range(4, STEPS + LAG):
            for load, number in later[:2]:
                load(number)
            later = later[2:]
            if step < STEPS:
                mix(step, (0,))
            if step <= STEPS:
                group_channels(step - 1)
            if step < STEPS:
                mix(step, (1,))
            units = ()
            if step < GROUPS[-1][0]:
                first, n = group_of(step)
                ratio = group_of(first + n)[1] // n
                units = range(first + n + ratio * (step - first), first + n + ratio * (step - first + 1))
            for unit in units:
                fold(unit)
                unfold(unit)
            if step <= STEPS:
                quantise_ctx(step - 1)
            project(step - LAG)
